import numpy as np
import ml_dtypes

BF16 = ml_dtypes.bfloat16


def bf(x):
    return np.asarray(x, np.float32).astype(BF16)


def f32(x):
    return np.asarray(x, np.float32)


def f64(x):
    return np.asarray(x).astype(np.float64)


def striped(idx):
    return np.tile(idx.reshape(-1, 16).T, (8, 1))


C, S, N = 256, 1024, 2048


def softplus(v):
    return np.log(1.0 + np.exp(v))


def setup_inputs():
    return {"emb": f32(np.random.uniform(size=(C, S))), "mix": f32(2.0 * np.random.standard_normal((C, N))), "cov_gamma": f32(0.4 * np.random.standard_normal((C, N))), "w2": bf(np.random.standard_normal((C, C)) / np.sqrt(C)), "b2": f32(0.1 * np.random.standard_normal((C, 1))), "w3": bf(np.random.standard_normal((C, C)) / np.sqrt(C)), "b3": f32(0.1 * np.random.standard_normal((C, 1))), "offs": striped(np.random.permutation(np.tile(np.arange(S), 2))[:N])}


def reference(emb, mix, cov_gamma, w2, b2, w3, b3, offs):
    idx = offs[:16].T.reshape(-1)
    h1 = softplus(f64(emb)[:, idx] * f64(mix) * (1.0 + f64(cov_gamma)))
    h2 = softplus(f64(w2).T @ h1 + f64(b2))
    return softplus(f64(w3).T @ h2 + f64(b3))

@@ -1,0 +1,95 @@
+import concourse.mybir as mybir
+
+F32 = mybir.dt.float32
+BF16 = mybir.dt.bfloat16
+U16 = mybir.dt.uint16
+ALU = mybir.AluOpType
+FUNC = mybir.ActivationFunctionType
+
+P = 128
+C, S, N = 256, 1024, 2048
+BLOCKS = C // P
+PIECE = 512
+PIECES = N // PIECE
+COLS = PIECE // 16
+
+CAP = 30.0
+
+FLOPS = 2 * 2 * C * C * N
+
+
+def log1p_exp(nc, work, capped):
+    grown = work.tile([P, PIECE], F32, name="grown")
+    nc.scalar.activation(grown[:], capped[:], FUNC.Exp)
+    log_term = work.tile([P, PIECE], F32, name="log_term")
+    nc.scalar.activation(log_term[:], grown[:], FUNC.Ln, bias=1.0)
+    return log_term
+
+
+def linear_softplus(nc, work, psum, weights, bias, h_in, m, result):
+    acc = psum.tile([P, PIECE], F32, name="acc")
+    for k in range(BLOCKS):
+        nc.tensor.matmul(
+            acc[:], weights[k][:, m * P : (m + 1) * P], h_in[k][:], start=(k == 0), stop=(k == BLOCKS - 1)
+        )
+    capped = work.tile([P, PIECE], F32, name="capped")
+    nc.vector.tensor_scalar(capped[:], acc[:], bias[m][:], CAP, op0=ALU.add, op1=ALU.min)
+    log_term = log1p_exp(nc, work, capped)
+    nc.vector.scalar_tensor_tensor(result[:], acc[:], bias[m][:], log_term[:], op0=ALU.add, op1=ALU.max)
+
+
+def tile_conditionalvelocitymodel_kernel(tc, emb, mix, cov_gamma, w2, b2, w3, b3, offs, out):
+    nc = tc.nc
+    with (
+        tc.tile_pool(name="held", bufs=1) as held,
+        tc.tile_pool(name="loads", bufs=BLOCKS * PIECES) as loads,
+        tc.tile_pool(name="work", bufs=4) as work,
+        tc.psum_pool(name="psum", bufs=8) as psum,
+    ):
+        offsets = held.tile([P, N // 16], U16, name="offsets")
+        nc.sync.dma_start(offsets[:], offs)
+        table = [held.tile([P, S], F32, name=f"table{b}") for b in range(BLOCKS)]
+        w2_rows = [held.tile([P, C], BF16, name=f"w2_rows{b}") for b in range(BLOCKS)]
+        w3_rows = [held.tile([P, C], BF16, name=f"w3_rows{b}") for b in range(BLOCKS)]
+        b2_col = [held.tile([P, 1], F32, name=f"b2_col{b}") for b in range(BLOCKS)]
+        b3_col = [held.tile([P, 1], F32, name=f"b3_col{b}") for b in range(BLOCKS)]
+        for b in range(BLOCKS):
+            rows = slice(b * P, (b + 1) * P)
+            nc.sync.dma_start(table[b][:], emb[rows, :])
+            nc.scalar.dma_start(w2_rows[b][:], w2[rows, :])
+            nc.scalar.dma_start(w3_rows[b][:], w3[rows, :])
+            nc.scalar.dma_start(b2_col[b][:], b2[rows, :])
+            nc.scalar.dma_start(b3_col[b][:], b3[rows, :])
+
+        for j in range(PIECES):
+            samples = slice(j * PIECE, (j + 1) * PIECE)
+
+            h1 = []
+            for b in range(BLOCKS):
+                rows = slice(b * P, (b + 1) * P)
+                mix_t = loads.tile([P, PIECE], F32, name="mix_t")
+                nc.sync.dma_start(mix_t[:], mix[rows, samples])
+                cov_t = loads.tile([P, PIECE], F32, name="cov_t")
+                nc.sync.dma_start(cov_t[:], cov_gamma[rows, samples])
+                factor = work.tile([P, PIECE], F32, name="factor")
+                nc.vector.scalar_tensor_tensor(factor[:], cov_t[:], 1.0, mix_t[:], op0=ALU.add, op1=ALU.mult)
+                scaled = work.tile([P, PIECE], F32, name="scaled")
+                picked = table[b][:].indirect(offsets[:, j * COLS : (j + 1) * COLS])
+                nc.vector.tensor_tensor(scaled[:], picked, factor[:], ALU.mult)
+                capped = work.tile([P, PIECE], F32, name="capped")
+                nc.vector.tensor_scalar_min(capped[:], scaled[:], CAP)
+                log_term = log1p_exp(nc, work, capped)
+                h1_b = work.tile([P, PIECE], BF16, name=f"h1_{b}")
+                nc.vector.tensor_tensor(h1_b[:], scaled[:], log_term[:], ALU.max)
+                h1.append(h1_b)
+
+            h2 = []
+            for m in range(BLOCKS):
+                h2_m = work.tile([P, PIECE], BF16, name=f"h2_{m}")
+                linear_softplus(nc, work, psum, w2_rows, b2_col, h1, m, h2_m)
+                h2.append(h2_m)
+
+            for m in range(BLOCKS):
+                result = work.tile([P, PIECE], F32, name="result")
+                linear_softplus(nc, work, psum, w3_rows, b3_col, h2, m, result)
+                nc.sync.dma_start(out[m * P : (m + 1) * P, samples], result[:])

@@ -12,38 +12,50 @@ BLOCKS = C // P
 PIECE = 512
 PIECES = N // PIECE
 COLS = PIECE // 16
+WIDE = BLOCKS * N
 
-CAP = 30.0
+BIG = 2.0**60
 
 FLOPS = 2 * 2 * C * C * N
 
 
-def log1p_exp(nc, work, capped):
-    grown = work.tile([P, PIECE], F32, name="grown")
-    nc.scalar.activation(grown[:], capped[:], FUNC.Exp)
-    log_term = work.tile([P, PIECE], F32, name="log_term")
-    nc.scalar.activation(log_term[:], grown[:], FUNC.Ln, bias=1.0)
-    return log_term
+def part(j, b):
+    start = (j * BLOCKS + b) * PIECE
+    return slice(start, start + PIECE)
 
 
-def linear_softplus(nc, work, psum, weights, bias, h_in, m, result):
-    acc = psum.tile([P, PIECE], F32, name="acc")
-    for k in range(BLOCKS):
-        nc.tensor.matmul(
-            acc[:], weights[k][:, m * P : (m + 1) * P], h_in[k][:], start=(k == 0), stop=(k == BLOCKS - 1)
-        )
-    capped = work.tile([P, PIECE], F32, name="capped")
-    nc.vector.tensor_scalar(capped[:], acc[:], bias[m][:], CAP, op0=ALU.add, op1=ALU.min)
-    log_term = log1p_exp(nc, work, capped)
-    nc.vector.scalar_tensor_tensor(result[:], acc[:], bias[m][:], log_term[:], op0=ALU.add, op1=ALU.max)
+def linear_softplus(nc, wide, psum, weights, bias, h_in, result):
+    grown = wide.tile([P, WIDE], F32, name="grown")
+    accs = {}
+    for j in range(PIECES):
+        for m in range(BLOCKS):
+            acc = psum.tile([P, PIECE], F32, name="acc")
+            for k in range(BLOCKS):
+                nc.tensor.matmul(
+                    acc[:],
+                    weights[k][:, m * P : (m + 1) * P],
+                    h_in[:, part(j, k)],
+                    start=(k == 0),
+                    stop=(k == BLOCKS - 1),
+                )
+            nc.scalar.activation(grown[:, part(j, m)], acc[:], FUNC.Exp, bias=bias[m][:])
+            accs[(j, m)] = acc
+    log_term = wide.tile([P, WIDE], F32, name="log_term")
+    for j in range(PIECES):
+        for m in range(BLOCKS):
+            here = part(j, m)
+            nc.vector.tensor_scalar_min(grown[:, here], grown[:, here], BIG)
+            nc.scalar.activation(log_term[:, here], grown[:, here], FUNC.Ln, bias=1.0)
+            nc.vector.scalar_tensor_tensor(
+                result[:, here], accs[(j, m)][:], bias[m][:], log_term[:, here], op0=ALU.add, op1=ALU.max
+            )
 
 
 def tile_conditionalvelocitymodel_kernel(tc, emb, mix, cov_gamma, w2, b2, w3, b3, offs, out):
     nc = tc.nc
     with (
         tc.tile_pool(name="held", bufs=1) as held,
-        tc.tile_pool(name="loads", bufs=BLOCKS * PIECES) as loads,
-        tc.tile_pool(name="work", bufs=4) as work,
+        tc.tile_pool(name="wide", bufs=2) as wide,
         tc.psum_pool(name="psum", bufs=8) as psum,
     ):
         offsets = held.tile([P, N // 16], U16, name="offsets")
@@ -53,43 +65,53 @@ def tile_conditionalvelocitymodel_kernel(tc, emb, mix, cov_gamma, w2, b2, w3, b3
         w3_rows = [held.tile([P, C], BF16, name=f"w3_rows{b}") for b in range(BLOCKS)]
         b2_col = [held.tile([P, 1], F32, name=f"b2_col{b}") for b in range(BLOCKS)]
         b3_col = [held.tile([P, 1], F32, name=f"b3_col{b}") for b in range(BLOCKS)]
-        for b in range(BLOCKS):
-            rows = slice(b * P, (b + 1) * P)
-            nc.sync.dma_start(table[b][:], emb[rows, :])
-            nc.scalar.dma_start(w2_rows[b][:], w2[rows, :])
-            nc.scalar.dma_start(w3_rows[b][:], w3[rows, :])
-            nc.scalar.dma_start(b2_col[b][:], b2[rows, :])
-            nc.scalar.dma_start(b3_col[b][:], b3[rows, :])
-
+        mix_all = held.tile([P, WIDE], F32, name="mix_all")
+        cov_all = held.tile([P, WIDE], F32, name="cov_all")
+        both = "(b p) s -> p b s"
         for j in range(PIECES):
             samples = slice(j * PIECE, (j + 1) * PIECE)
+            pair = slice(j * BLOCKS * PIECE, (j + 1) * BLOCKS * PIECE)
+            nc.sync.dma_start(
+                mix_all[:, pair].rearrange("p (b s) -> p b s", b=BLOCKS), mix[:, samples].rearrange(both, p=P)
+            )
+            nc.sync.dma_start(
+                cov_all[:, pair].rearrange("p (b s) -> p b s", b=BLOCKS), cov_gamma[:, samples].rearrange(both, p=P)
+            )
+            if j == 0:
+                for b in range(BLOCKS):
+                    nc.sync.dma_start(table[b][:], emb[b * P : (b + 1) * P, :])
+        for b in range(BLOCKS):
+            rows = slice(b * P, (b + 1) * P)
+            nc.sync.dma_start(w2_rows[b][:], w2[rows, :])
+            nc.sync.dma_start(w3_rows[b][:], w3[rows, :])
+            nc.sync.dma_start(b2_col[b][:], b2[rows, :])
+            nc.sync.dma_start(b3_col[b][:], b3[rows, :])
 
-            h1 = []
+        factor = held.tile([P, WIDE], F32, name="factor", tag="factor_then_log")
+        scaled = held.tile([P, WIDE], F32, name="scaled")
+        grown = wide.tile([P, WIDE], F32, name="grown")
+        for j in range(PIECES):
             for b in range(BLOCKS):
-                rows = slice(b * P, (b + 1) * P)
-                mix_t = loads.tile([P, PIECE], F32, name="mix_t")
-                nc.sync.dma_start(mix_t[:], mix[rows, samples])
-                cov_t = loads.tile([P, PIECE], F32, name="cov_t")
-                nc.sync.dma_start(cov_t[:], cov_gamma[rows, samples])
-                factor = work.tile([P, PIECE], F32, name="factor")
-                nc.vector.scalar_tensor_tensor(factor[:], cov_t[:], 1.0, mix_t[:], op0=ALU.add, op1=ALU.mult)
-                scaled = work.tile([P, PIECE], F32, name="scaled")
+                here = part(j, b)
+                nc.vector.scalar_tensor_tensor(
+                    factor[:, here], cov_all[:, here], 1.0, mix_all[:, here], op0=ALU.add, op1=ALU.mult
+                )
                 picked = table[b][:].indirect(offsets[:, j * COLS : (j + 1) * COLS])
-                nc.vector.tensor_tensor(scaled[:], picked, factor[:], ALU.mult)
-                capped = work.tile([P, PIECE], F32, name="capped")
-                nc.vector.tensor_scalar_min(capped[:], scaled[:], CAP)
-                log_term = log1p_exp(nc, work, capped)
-                h1_b = work.tile([P, PIECE], BF16, name=f"h1_{b}")
-                nc.vector.tensor_tensor(h1_b[:], scaled[:], log_term[:], ALU.max)
-                h1.append(h1_b)
+                nc.vector.tensor_tensor(scaled[:, here], picked, factor[:, here], ALU.mult)
+                nc.scalar.activation(grown[:, here], scaled[:, here], FUNC.Exp)
+        log_term = held.tile([P, WIDE], F32, name="log_term", tag="factor_then_log")
+        h1 = held.tile([P, WIDE], BF16, name="h1")
+        for j in range(PIECES):
+            for b in range(BLOCKS):
+                here = part(j, b)
+                nc.vector.tensor_scalar_min(grown[:, here], grown[:, here], BIG)
+                nc.scalar.activation(log_term[:, here], grown[:, here], FUNC.Ln, bias=1.0)
+                nc.vector.tensor_tensor(h1[:, here], scaled[:, here], log_term[:, here], ALU.max)
 
-            h2 = []
+        h2 = held.tile([P, WIDE], BF16, name="h2")
+        linear_softplus(nc, wide, psum, w2_rows, b2_col, h1, h2)
+        result = held.tile([P, WIDE], F32, name="result")
+        linear_softplus(nc, wide, psum, w3_rows, b3_col, h2, result)
+        for j in range(PIECES):
             for m in range(BLOCKS):
-                h2_m = work.tile([P, PIECE], BF16, name=f"h2_{m}")
-                linear_softplus(nc, work, psum, w2_rows, b2_col, h1, m, h2_m)
-                h2.append(h2_m)
-
-            for m in range(BLOCKS):
-                result = work.tile([P, PIECE], F32, name="result")
-                linear_softplus(nc, work, psum, w3_rows, b3_col, h2, m, result)
-                nc.sync.dma_start(out[m * P : (m + 1) * P, samples], result[:])
+                nc.sync.dma_start(out[m * P : (m + 1) * P, j * PIECE : (j + 1) * PIECE], result[:, part(j, m)])

@@ -13,8 +13,10 @@ PIECE = 512
 PIECES = N // PIECE
 COLS = PIECE // 16
 WIDE = BLOCKS * N
+HALF = WIDE // 2
 
 BIG = 2.0**60
+CAP = 41.0
 
 FLOPS = 2 * 2 * C * C * N
 
@@ -24,7 +26,7 @@ def part(j, b):
     return slice(start, start + PIECE)
 
 
-def linear_softplus(nc, wide, psum, weights, bias, h_in, result):
+def linear_softplus(nc, held, wide, psum, weights, bias, h_in, result):
     grown = wide.tile([P, WIDE], F32, name="grown")
     accs = {}
     for j in range(PIECES):
@@ -67,8 +69,13 @@ def tile_conditionalvelocitymodel_kernel(tc, emb, mix, cov_gamma, w2, b2, w3, b3
         b3_col = [held.tile([P, 1], F32, name=f"b3_col{b}") for b in range(BLOCKS)]
         mix_all = held.tile([P, WIDE], F32, name="mix_all")
         cov_all = held.tile([P, WIDE], F32, name="cov_all")
+        for b in range(BLOCKS):
+            rows = slice(b * P, (b + 1) * P)
+            nc.sync.dma_start(table[b][:], emb[rows, :])
+            nc.sync.dma_start(mix_all[:, part(0, b)], mix[rows, 0:PIECE])
+            nc.sync.dma_start(cov_all[:, part(0, b)], cov_gamma[rows, 0:PIECE])
         both = "(b p) s -> p b s"
-        for j in range(PIECES):
+        for j in range(1, PIECES):
             samples = slice(j * PIECE, (j + 1) * PIECE)
             pair = slice(j * BLOCKS * PIECE, (j + 1) * BLOCKS * PIECE)
             nc.sync.dma_start(
@@ -77,9 +84,6 @@ def tile_conditionalvelocitymodel_kernel(tc, emb, mix, cov_gamma, w2, b2, w3, b3
             nc.sync.dma_start(
                 cov_all[:, pair].rearrange("p (b s) -> p b s", b=BLOCKS), cov_gamma[:, samples].rearrange(both, p=P)
             )
-            if j == 0:
-                for b in range(BLOCKS):
-                    nc.sync.dma_start(table[b][:], emb[b * P : (b + 1) * P, :])
         for b in range(BLOCKS):
             rows = slice(b * P, (b + 1) * P)
             nc.sync.dma_start(w2_rows[b][:], w2[rows, :])
@@ -87,31 +91,36 @@ def tile_conditionalvelocitymodel_kernel(tc, emb, mix, cov_gamma, w2, b2, w3, b3
             nc.sync.dma_start(b2_col[b][:], b2[rows, :])
             nc.sync.dma_start(b3_col[b][:], b3[rows, :])
 
-        factor = held.tile([P, WIDE], F32, name="factor", tag="factor_then_log")
         scaled = held.tile([P, WIDE], F32, name="scaled")
         grown = wide.tile([P, WIDE], F32, name="grown")
+        log_term = wide.tile([P, WIDE], F32, name="log_term")
+        products = [held.tile([P, HALF], F32, name=f"product{half}") for half in range(2)]
+        for half in range(2):
+            first = half * (PIECES // 2)
+            for j in range(first, first + PIECES // 2):
+                for b in range(BLOCKS):
+                    here = part(j, b)
+                    there = part(j - first, b)
+                    picked = table[b][:].indirect(offsets[:, j * COLS : (j + 1) * COLS])
+                    nc.vector.tensor_tensor(products[half][:, there], picked, mix_all[:, here], ALU.mult)
+                    nc.vector.scalar_tensor_tensor(
+                        scaled[:, here], cov_all[:, here], 1.0, products[half][:, there], op0=ALU.add, op1=ALU.mult
+                    )
+                    nc.scalar.activation(grown[:, here], scaled[:, here], FUNC.Exp)
+            whole_half = slice(half * HALF, (half + 1) * HALF)
+            nc.scalar.activation(log_term[:, whole_half], grown[:, whole_half], FUNC.Ln, bias=1.0)
+        h1 = held.tile([P, WIDE], BF16, name="h1", tag="product1")
         for j in range(PIECES):
             for b in range(BLOCKS):
                 here = part(j, b)
                 nc.vector.scalar_tensor_tensor(
-                    factor[:, here], cov_all[:, here], 1.0, mix_all[:, here], op0=ALU.add, op1=ALU.mult
+                    h1[:, here], log_term[:, here], CAP, scaled[:, here], op0=ALU.min, op1=ALU.max
                 )
-                picked = table[b][:].indirect(offsets[:, j * COLS : (j + 1) * COLS])
-                nc.vector.tensor_tensor(scaled[:, here], picked, factor[:, here], ALU.mult)
-                nc.scalar.activation(grown[:, here], scaled[:, here], FUNC.Exp)
-        log_term = held.tile([P, WIDE], F32, name="log_term", tag="factor_then_log")
-        h1 = held.tile([P, WIDE], BF16, name="h1")
-        for j in range(PIECES):
-            for b in range(BLOCKS):
-                here = part(j, b)
-                nc.vector.tensor_scalar_min(grown[:, here], grown[:, here], BIG)
-                nc.scalar.activation(log_term[:, here], grown[:, here], FUNC.Ln, bias=1.0)
-                nc.vector.tensor_tensor(h1[:, here], scaled[:, here], log_term[:, here], ALU.max)
 
         h2 = held.tile([P, WIDE], BF16, name="h2")
-        linear_softplus(nc, wide, psum, w2_rows, b2_col, h1, h2)
+        linear_softplus(nc, held, wide, psum, w2_rows, b2_col, h1, h2)
         result = held.tile([P, WIDE], F32, name="result")
-        linear_softplus(nc, wide, psum, w3_rows, b3_col, h2, result)
+        linear_softplus(nc, held, wide, psum, w3_rows, b3_col, h2, result)
         for j in range(PIECES):
             for m in range(BLOCKS):
                 nc.sync.dma_start(out[m * P : (m + 1) * P, j * PIECE : (j + 1) * PIECE], result[:, part(j, m)])

@@ -14,6 +14,7 @@ PIECES = N // PIECE
 COLS = PIECE // 16
 WIDE = BLOCKS * N
 HALF = WIDE // 2
+LAST_CUTS = 2
 
 BIG = 2.0**60
 CAP = 41.0
@@ -26,7 +27,7 @@ def part(j, b):
     return slice(start, start + PIECE)
 
 
-def linear_softplus(nc, held, wide, psum, weights, bias, h_in, result):
+def linear_softplus(nc, held, wide, psum, weights, bias, h_in, result, cuts):
     grown = wide.tile([P, WIDE], F32, name="grown")
     accs = {}
     for j in range(PIECES):
@@ -45,12 +46,20 @@ def linear_softplus(nc, held, wide, psum, weights, bias, h_in, result):
     log_term = wide.tile([P, WIDE], F32, name="log_term")
     for j in range(PIECES):
         for m in range(BLOCKS):
-            here = part(j, m)
-            nc.vector.tensor_scalar_min(grown[:, here], grown[:, here], BIG)
-            nc.scalar.activation(log_term[:, here], grown[:, here], FUNC.Ln, bias=1.0)
-            nc.vector.scalar_tensor_tensor(
-                result[:, here], accs[(j, m)][:], bias[m][:], log_term[:, here], op0=ALU.add, op1=ALU.max
-            )
+            whole = part(j, m)
+            nc.vector.tensor_scalar_min(grown[:, whole], grown[:, whole], BIG)
+            width = PIECE // cuts
+            for c in range(cuts):
+                here = slice(whole.start + c * width, whole.start + (c + 1) * width)
+                nc.scalar.activation(log_term[:, here], grown[:, here], FUNC.Ln, bias=1.0)
+                nc.vector.scalar_tensor_tensor(
+                    result[:, here],
+                    accs[(j, m)][:, c * width : (c + 1) * width],
+                    bias[m][:],
+                    log_term[:, here],
+                    op0=ALU.add,
+                    op1=ALU.max,
+                )
 
 
 def tile_conditionalvelocitymodel_kernel(tc, emb, mix, cov_gamma, w2, b2, w3, b3, offs, out):
@@ -118,9 +127,14 @@ def tile_conditionalvelocitymodel_kernel(tc, emb, mix, cov_gamma, w2, b2, w3, b3
                 )
 
         h2 = held.tile([P, WIDE], BF16, name="h2")
-        linear_softplus(nc, held, wide, psum, w2_rows, b2_col, h1, h2)
+        linear_softplus(nc, held, wide, psum, w2_rows, b2_col, h1, h2, cuts=1)
         result = held.tile([P, WIDE], F32, name="result")
-        linear_softplus(nc, held, wide, psum, w3_rows, b3_col, h2, result)
+        linear_softplus(nc, held, wide, psum, w3_rows, b3_col, h2, result, cuts=LAST_CUTS)
+        width = PIECE // LAST_CUTS
         for j in range(PIECES):
             for m in range(BLOCKS):
-                nc.sync.dma_start(out[m * P : (m + 1) * P, j * PIECE : (j + 1) * PIECE], result[:, part(j, m)])
+                for c in range(LAST_CUTS):
+                    nc.sync.dma_start(
+                        out[m * P : (m + 1) * P, j * PIECE + c * width : j * PIECE + (c + 1) * width],
+                        result[:, part(j, m).start + c * width : part(j, m).start + (c + 1) * width],
+                    )

@@ -13,7 +13,6 @@ PIECE = 512
 PIECES = N // PIECE
 COLS = PIECE // 16
 WIDE = BLOCKS * N
-HALF = WIDE // 2
 LAST_CUTS = 2
 
 BIG = 2.0**60
@@ -23,7 +22,7 @@ FLOPS = 2 * 2 * C * C * N
 
 
 def part(j, b):
-    start = (j * BLOCKS + b) * PIECE
+    start = (b * PIECES + j) * PIECE
     return slice(start, start + PIECE)
 
 
@@ -81,18 +80,13 @@ def tile_conditionalvelocitymodel_kernel(tc, emb, mix, cov_gamma, w2, b2, w3, b3
         for b in range(BLOCKS):
             rows = slice(b * P, (b + 1) * P)
             nc.sync.dma_start(table[b][:], emb[rows, :])
-            nc.sync.dma_start(mix_all[:, part(0, b)], mix[rows, 0:PIECE])
-            nc.sync.dma_start(cov_all[:, part(0, b)], cov_gamma[rows, 0:PIECE])
-        both = "(b p) s -> p b s"
-        for j in range(1, PIECES):
-            samples = slice(j * PIECE, (j + 1) * PIECE)
-            pair = slice(j * BLOCKS * PIECE, (j + 1) * BLOCKS * PIECE)
-            nc.sync.dma_start(
-                mix_all[:, pair].rearrange("p (b s) -> p b s", b=BLOCKS), mix[:, samples].rearrange(both, p=P)
-            )
-            nc.sync.dma_start(
-                cov_all[:, pair].rearrange("p (b s) -> p b s", b=BLOCKS), cov_gamma[:, samples].rearrange(both, p=P)
-            )
+            for first in range(0, PIECES, 2):
+                step = 1 if (b == 0 and first == 0) else 2
+                for j in range(first, first + 2, step):
+                    samples = slice(j * PIECE, (j + step) * PIECE)
+                    here = slice(part(j, b).start, part(j, b).start + step * PIECE)
+                    nc.sync.dma_start(mix_all[:, here], mix[rows, samples])
+                    nc.sync.dma_start(cov_all[:, here], cov_gamma[rows, samples])
         for b in range(BLOCKS):
             rows = slice(b * P, (b + 1) * P)
             nc.sync.dma_start(w2_rows[b][:], w2[rows, :])
@@ -103,24 +97,22 @@ def tile_conditionalvelocitymodel_kernel(tc, emb, mix, cov_gamma, w2, b2, w3, b3
         scaled = held.tile([P, WIDE], F32, name="scaled")
         grown = wide.tile([P, WIDE], F32, name="grown")
         log_term = wide.tile([P, WIDE], F32, name="log_term")
-        products = [held.tile([P, HALF], F32, name=f"product{half}") for half in range(2)]
-        for half in range(2):
-            first = half * (PIECES // 2)
-            for j in range(first, first + PIECES // 2):
-                for b in range(BLOCKS):
-                    here = part(j, b)
-                    there = part(j - first, b)
-                    picked = table[b][:].indirect(offsets[:, j * COLS : (j + 1) * COLS])
-                    nc.vector.tensor_tensor(products[half][:, there], picked, mix_all[:, here], ALU.mult)
-                    nc.vector.scalar_tensor_tensor(
-                        scaled[:, here], cov_all[:, here], 1.0, products[half][:, there], op0=ALU.add, op1=ALU.mult
-                    )
-                    nc.scalar.activation(grown[:, here], scaled[:, here], FUNC.Exp)
-            whole_half = slice(half * HALF, (half + 1) * HALF)
-            nc.scalar.activation(log_term[:, whole_half], grown[:, whole_half], FUNC.Ln, bias=1.0)
+        products = [held.tile([P, N], F32, name=f"product{b}") for b in range(BLOCKS)]
+        for b in range(BLOCKS):
+            for j in range(PIECES):
+                here = part(j, b)
+                samples = slice(j * PIECE, (j + 1) * PIECE)
+                picked = table[b][:].indirect(offsets[:, j * COLS : (j + 1) * COLS])
+                nc.vector.tensor_tensor(products[b][:, samples], picked, mix_all[:, here], ALU.mult)
+                nc.vector.scalar_tensor_tensor(
+                    scaled[:, here], cov_all[:, here], 1.0, products[b][:, samples], op0=ALU.add, op1=ALU.mult
+                )
+                nc.scalar.activation(grown[:, here], scaled[:, here], FUNC.Exp)
+            whole_block = slice(b * N, (b + 1) * N)
+            nc.scalar.activation(log_term[:, whole_block], grown[:, whole_block], FUNC.Ln, bias=1.0)
         h1 = held.tile([P, WIDE], BF16, name="h1", tag="product1")
-        for j in range(PIECES):
-            for b in range(BLOCKS):
+        for b in range(BLOCKS):
+            for j in range(PIECES):
                 here = part(j, b)
                 nc.vector.scalar_tensor_tensor(
                     h1[:, here], log_term[:, here], CAP, scaled[:, here], op0=ALU.min, op1=ALU.max

import concourse.mybir as mybir

F32 = mybir.dt.float32
BF16 = mybir.dt.bfloat16
U16 = mybir.dt.uint16
ALU = mybir.AluOpType
FUNC = mybir.ActivationFunctionType

P = 128
C, S, N = 256, 1024, 2048
BLOCKS = C // P
PIECE = 512
PIECES = N // PIECE
COLS = PIECE // 16
WIDE = BLOCKS * N
LAST_CUTS = 2

BIG = 2.0**60
CAP = 41.0

FLOPS = 2 * 2 * C * C * N


def part(j, b):
    start = (b * PIECES + j) * PIECE
    return slice(start, start + PIECE)


def linear_softplus(nc, held, wide, psum, weights, bias, h_in, result, cuts):
    grown = wide.tile([P, WIDE], F32, name="grown")
    accs = {}
    for j in range(PIECES):
        for m in range(BLOCKS):
            acc = psum.tile([P, PIECE], F32, name="acc")
            for k in range(BLOCKS):
                nc.tensor.matmul(
                    acc[:],
                    weights[k][:, m * P : (m + 1) * P],
                    h_in[:, part(j, k)],
                    start=(k == 0),
                    stop=(k == BLOCKS - 1),
                )
            nc.scalar.activation(grown[:, part(j, m)], acc[:], FUNC.Exp, bias=bias[m][:])
            accs[(j, m)] = acc
    log_term = wide.tile([P, WIDE], F32, name="log_term")
    for j in range(PIECES):
        for m in range(BLOCKS):
            whole = part(j, m)
            nc.vector.tensor_scalar_min(grown[:, whole], grown[:, whole], BIG)
            width = PIECE // cuts
            for c in range(cuts):
                here = slice(whole.start + c * width, whole.start + (c + 1) * width)
                nc.scalar.activation(log_term[:, here], grown[:, here], FUNC.Ln, bias=1.0)
                nc.vector.scalar_tensor_tensor(
                    result[:, here],
                    accs[(j, m)][:, c * width : (c + 1) * width],
                    bias[m][:],
                    log_term[:, here],
                    op0=ALU.add,
                    op1=ALU.max,
                )


def tile_conditionalvelocitymodel_kernel(tc, emb, mix, cov_gamma, w2, b2, w3, b3, offs, out):
    nc = tc.nc
    with (
        tc.tile_pool(name="held", bufs=1) as held,
        tc.tile_pool(name="wide", bufs=2) as wide,
        tc.psum_pool(name="psum", bufs=8) as psum,
    ):
        offsets = held.tile([P, N // 16], U16, name="offsets")
        nc.sync.dma_start(offsets[:], offs)
        table = [held.tile([P, S], F32, name=f"table{b}") for b in range(BLOCKS)]
        w2_rows = [held.tile([P, C], BF16, name=f"w2_rows{b}") for b in range(BLOCKS)]
        w3_rows = [held.tile([P, C], BF16, name=f"w3_rows{b}") for b in range(BLOCKS)]
        b2_col = [held.tile([P, 1], F32, name=f"b2_col{b}") for b in range(BLOCKS)]
        b3_col = [held.tile([P, 1], F32, name=f"b3_col{b}") for b in range(BLOCKS)]
        mix_all = held.tile([P, WIDE], F32, name="mix_all")
        cov_all = held.tile([P, WIDE], F32, name="cov_all")
        for b in range(BLOCKS):
            rows = slice(b * P, (b + 1) * P)
            nc.sync.dma_start(table[b][:], emb[rows, :])
            for first in range(0, PIECES, 2):
                step = 1 if (b == 0 and first == 0) else 2
                for j in range(first, first + 2, step):
                    samples = slice(j * PIECE, (j + step) * PIECE)
                    here = slice(part(j, b).start, part(j, b).start + step * PIECE)
                    nc.sync.dma_start(mix_all[:, here], mix[rows, samples])
                    nc.sync.dma_start(cov_all[:, here], cov_gamma[rows, samples])
        for b in range(BLOCKS):
            rows = slice(b * P, (b + 1) * P)
            nc.sync.dma_start(w2_rows[b][:], w2[rows, :])
            nc.sync.dma_start(w3_rows[b][:], w3[rows, :])
            nc.sync.dma_start(b2_col[b][:], b2[rows, :])
            nc.sync.dma_start(b3_col[b][:], b3[rows, :])

        scaled = held.tile([P, WIDE], F32, name="scaled")
        grown = wide.tile([P, WIDE], F32, name="grown")
        log_term = wide.tile([P, WIDE], F32, name="log_term")
        products = [held.tile([P, N], F32, name=f"product{b}") for b in range(BLOCKS)]
        for b in range(BLOCKS):
            for j in range(PIECES):
                here = part(j, b)
                samples = slice(j * PIECE, (j + 1) * PIECE)
                picked = table[b][:].indirect(offsets[:, j * COLS : (j + 1) * COLS])
                nc.vector.tensor_tensor(products[b][:, samples], picked, mix_all[:, here], ALU.mult)
                nc.vector.scalar_tensor_tensor(
                    scaled[:, here], cov_all[:, here], 1.0, products[b][:, samples], op0=ALU.add, op1=ALU.mult
                )
                nc.scalar.activation(grown[:, here], scaled[:, here], FUNC.Exp)
            whole_block = slice(b * N, (b + 1) * N)
            nc.scalar.activation(log_term[:, whole_block], grown[:, whole_block], FUNC.Ln, bias=1.0)
        h1 = held.tile([P, WIDE], BF16, name="h1", tag="product1")
        for b in range(BLOCKS):
            for j in range(PIECES):
                here = part(j, b)
                nc.vector.scalar_tensor_tensor(
                    h1[:, here], log_term[:, here], CAP, scaled[:, here], op0=ALU.min, op1=ALU.max
                )

        h2 = held.tile([P, WIDE], BF16, name="h2")
        linear_softplus(nc, held, wide, psum, w2_rows, b2_col, h1, h2, cuts=1)
        result = held.tile([P, WIDE], F32, name="result")
        linear_softplus(nc, held, wide, psum, w3_rows, b3_col, h2, result, cuts=LAST_CUTS)
        width = PIECE // LAST_CUTS
        for j in range(PIECES):
            for m in range(BLOCKS):
                for c in range(LAST_CUTS):
                    nc.sync.dma_start(
                        out[m * P : (m + 1) * P, j * PIECE + c * width : j * PIECE + (c + 1) * width],
                        result[:, part(j, m).start + c * width : part(j, m).start + (c + 1) * width],
                    )
